import numpy as np
import ml_dtypes


def mxq(x, axis, fmt="e4m3"):
    dtype, down = {"e4m3": (ml_dtypes.float8_e4m3fn, 7), "e5m2": (ml_dtypes.float8_e5m2, 14)}[fmt]
    v = np.moveaxis(np.asarray(x, np.float32).astype(ml_dtypes.bfloat16).astype(np.float64), axis, -1)
    blocks = v.reshape(v.shape[:-1] + (-1, 32))
    amax = np.abs(blocks).max(-1, keepdims=True)
    byte = np.maximum(np.where(amax > 0, np.frexp(amax)[1] - 1 + 127, 0) - down, 1)
    scale = np.exp2(byte - 127.0)
    codes = (blocks / scale).astype(np.float32).astype(dtype).astype(np.float64)
    return np.moveaxis((codes * scale).reshape(v.shape), -1, axis)


WIDE = False


def mx_kscale(k):
    if not WIDE:
        return np.ones(k)
    levels = np.array([10, -10, 5, -5, 0])
    a = np.random.permutation(np.resize(levels, k // 512 * 4)).reshape(k // 512, 4)
    idx = np.arange(k)
    return np.exp2(a[idx // 512, idx % 128 // 32])


BF16 = ml_dtypes.bfloat16


def bf(x):
    return np.asarray(x, np.float32).astype(BF16)


def f64(x):
    return np.asarray(x).astype(np.float64)


E2M1 = np.array([0.0, 0.5, 1.0, 1.5, 2.0, 3.0, 4.0, 6.0, -0.0, -0.5, -1.0, -1.5, -2.0, -3.0, -4.0, -6.0])


def pack_weight(w, fmt):
    k, n = w.shape
    w = f64(bf(w)).reshape(k // 32, 32, n)
    amax = np.abs(w).max(1)
    if fmt == "e4m3":
        byte = np.frexp(amax)[1] - 1 + 127 - 7
    else:
        mant, ex = np.frexp(amax / 6.0)
        byte = np.where(mant > 0.5, ex, ex - 1) + 127
    byte = np.clip(np.where(amax > 0, byte, 1), 1, 254)
    scaled = (w * np.exp2(127.0 - byte)[:, None, :]).reshape(k, n).astype(np.float32)
    by_word = np.ascontiguousarray(scaled.reshape(k // 512, 128, 4, n).transpose(0, 1, 3, 2))
    if fmt == "e4m3":
        words = by_word.astype(ml_dtypes.float8_e4m3fn).view(np.uint8)
    else:
        c = by_word.astype(ml_dtypes.float4_e2m1fn).view(np.uint8) & 0xF
        words = c[..., 0::2] | (c[..., 1::2] << 4)
    return np.ascontiguousarray(words), np.ascontiguousarray(byte.astype(np.uint8).reshape(k // 512, 16, n))


def unpack_weight(words, scales, fmt):
    g, p, n, _ = words.shape
    if fmt == "e4m3":
        vals = np.ascontiguousarray(words).view(ml_dtypes.float8_e4m3fn).astype(np.float64)
    else:
        nib = np.empty((g, p, n, 4), np.uint8)
        nib[..., 0::2] = words & 0xF
        nib[..., 1::2] = words >> 4
        vals = E2M1[nib]
    vals = vals * np.repeat(np.exp2(scales.astype(np.float64) - 127.0), 8, axis=1)[..., None]
    return vals.transpose(0, 1, 3, 2).reshape(g * 512, n)


B, D_IN, D_H, C = 256, 16384, 512, 128
TAU, T1, T2 = 0.5, 3, 3
G, GB = 3.0, 3.0
FMT = "e4m3"


def inv_apprx(v, t, m):
    a = 2.0 - (2.0 / m) * v
    b = 1.0 - (2.0 / m) * v
    for _ in range(t):
        b = b * b
        a = a * (1.0 + b)
    return (2.0 / m) * a


def comp_max_tau(p, tau, t1, t2):
    res = np.concatenate([p, np.full((p.shape[0], 1), tau)], axis=1)
    for i in range(t1):
        res = res * res
        sum_res = res.sum(axis=1)
        m = (2.0 + tau * tau) if i == 0 else 2.0
        res = res * inv_apprx(sum_res, t2, m)[:, None]
    return res[:, -1]


def softmax(z):
    e = np.exp(z - z.max(-1, keepdims=True))
    return e / e.sum(-1, keepdims=True)


def mlp(xq, W1_words, W1_scales, b1, W2_words, W2_scales, b2):
    h = np.maximum((xq @ unpack_weight(W1_words, W1_scales, FMT)) + f64(b1), 0.0)
    return softmax((mxq(h, 1, "e4m3") @ unpack_weight(W2_words, W2_scales, FMT)) + f64(b2))


def setup_inputs():
    s, t = mx_kscale(D_IN), mx_kscale(D_H)
    x = bf(np.random.standard_normal((B, D_IN)) * s)
    W1o_words, W1o_scales = pack_weight(np.random.standard_normal((D_IN, D_H)) / np.sqrt(D_IN) / s[:, None] * t, FMT)
    b1o = bf(np.random.standard_normal(D_H) * 0.2 * t)
    W2o_words, W2o_scales = pack_weight(np.random.standard_normal((D_H, C)) * G / np.sqrt(D_H) / t[:, None], FMT)
    b2o = bf(np.random.standard_normal(C) * GB)
    W1f_words, W1f_scales = pack_weight(np.random.standard_normal((D_IN, D_H)) / np.sqrt(D_IN) / s[:, None] * t, FMT)
    b1f = bf(np.random.standard_normal(D_H) * 0.2 * t)
    W2f_words, W2f_scales = pack_weight(np.random.standard_normal((D_H, C)) * G / np.sqrt(D_H) / t[:, None], FMT)
    b2f = bf(np.random.standard_normal(C) * GB)
    return {"x": x,
            "W1o_words": W1o_words, "W1o_scales": W1o_scales,
            "b1o": b1o,
            "W2o_words": W2o_words, "W2o_scales": W2o_scales,
            "b2o": b2o,
            "W1f_words": W1f_words, "W1f_scales": W1f_scales,
            "b1f": b1f,
            "W2f_words": W2f_words, "W2f_scales": W2f_scales,
            "b2f": b2f}


def reference(x, W1o_words, W1o_scales, b1o, W2o_words, W2o_scales, b2o, W1f_words, W1f_scales, b1f, W2f_words, W2f_scales, b2f):
    xq = mxq(f64(x), 1, "e4m3")
    x1 = mlp(xq, W1o_words, W1o_scales, b1o, W2o_words, W2o_scales, b2o)
    x2 = mlp(xq, W1f_words, W1f_scales, b1f, W2f_words, W2f_scales, b2f)
    cond_in = comp_max_tau(x1, TAU, T1, T2)
    return x1 * (1.0 - cond_in[:, None]) + x2 * cond_in[:, None]

@@ -1,0 +1,335 @@
+from contextlib import ExitStack
+
+import concourse.mybir as mybir
+from concourse.masks import make_identity
+
+F32 = mybir.dt.float32
+BF16 = mybir.dt.bfloat16
+I32 = mybir.dt.int32
+U32 = mybir.dt.uint32
+U8 = mybir.dt.uint8
+FP8X4 = mybir.dt.float8_e4m3fn_x4
+ALU = mybir.AluOpType
+ACT = mybir.ActivationFunctionType
+AXIS = mybir.AxisListType
+
+P = 128
+PACK = 4
+K_PASS = P * PACK
+BATCH = 256
+D_IN = 16384
+D_H = 512
+CLASSES = 128
+ROW_TILES = BATCH // P
+PASSES = D_IN // K_PASS
+ROUND = 4
+ROUNDS = PASSES // ROUND
+QUADRANTS = 4
+NETS = ("o", "f")
+TAU = 0.5
+GATE_ROUNDS = 3
+INVERSE_STEPS = 3
+
+FLOPS = 2 * BATCH * D_IN * D_H * 2 + 2 * BATCH * D_H * CLASSES * 2
+
+
+def tile_combnethe_pa_k_kernel(
+    tc, x, W1o_words, W1o_scales, b1o, W2o_words, W2o_scales, b2o,
+    W1f_words, W1f_scales, b1f, W2f_words, W2f_scales, b2f, out,
+):
+    nc = tc.nc
+    w1_words = {"o": W1o_words, "f": W1f_words}
+    w1_scales = {"o": W1o_scales, "f": W1f_scales}
+    w2_words = {"o": W2o_words, "f": W2f_words}
+    w2_scales = {"o": W2o_scales, "f": W2f_scales}
+
+    with ExitStack() as ctx:
+        ctx.enter_context(tc.manual_schedule())
+        keep = ctx.enter_context(tc.tile_pool(name="keep", bufs=1))
+        x_pool = ctx.enter_context(tc.tile_pool(name="x_pool", bufs=4))
+        w_pool = ctx.enter_context(tc.tile_pool(name="w_pool", bufs=10))
+        grouped_pool = ctx.enter_context(tc.tile_pool(name="grouped_pool", bufs=2))
+        psum_acc = ctx.enter_context(tc.psum_pool(name="psum_acc", bufs=1))
+        psum_bank = ctx.enter_context(tc.psum_pool(name="psum_bank", bufs=4))
+
+        w1_planes = {}
+        for net in NETS:
+            w1_planes[net] = keep.tile([P, ROUNDS * D_H], U8, name="w1_planes_" + net, align_bytes=64)
+        nc.vector.memset(w1_planes["o"][:].bitcast(I32), 0)
+
+        ident_f32 = keep.tile([P, P], F32, name="ident_f32")
+        make_identity(nc, ident_f32[:])
+        ident_bf16 = keep.tile([P, P], BF16, name="ident_bf16")
+        make_identity(nc, ident_bf16[:])
+
+        bias_rows = keep.tile([P, 2 * D_H + 2 * CLASSES], BF16, name="bias_rows")
+        nc.vector.memset(bias_rows[:], 0.0)
+        ones = keep.tile([P, P], BF16, name="ones")
+        nc.vector.memset(ones[:], 1.0)
+        nc.scalar.dma_start(out=bias_rows[0:1, 0:D_H], in_=b1o.rearrange("(a n) -> a n", a=1))
+        nc.scalar.dma_start(out=bias_rows[0:1, D_H:2 * D_H], in_=b1f.rearrange("(a n) -> a n", a=1))
+        nc.scalar.dma_start(
+            out=bias_rows[0:1, 2 * D_H:2 * D_H + CLASSES], in_=b2o.rearrange("(a n) -> a n", a=1)
+        )
+        nc.scalar.dma_start(
+            out=bias_rows[0:1, 2 * D_H + CLASSES:2 * D_H + 2 * CLASSES], in_=b2f.rearrange("(a n) -> a n", a=1)
+        )
+
+        w2_planes = keep.tile([P, 2 * CLASSES], U8, name="w2_planes", align_bytes=64)
+        nc.vector.memset(w2_planes[:].bitcast(I32), 0)
+        nc.vector.memset(w1_planes["f"][:].bitcast(I32), 0)
+        gate_last = keep.tile([P, ROW_TILES], F32, name="gate_last")
+        nc.vector.memset(gate_last[:], TAU)
+
+        b1_sb = {}
+        for i, net in enumerate(NETS):
+            spread1 = psum_bank.tile([P, D_H], F32, name="spread1", tag="bank")
+            nc.tensor.matmul(
+                out=spread1[:], lhsT=ones[:], rhs=bias_rows[:, i * D_H:(i + 1) * D_H], start=True, stop=True
+            )
+            b1_sb[net] = keep.tile([P, PACK, P], F32, name="b1_" + net)
+            nc.vector.tensor_copy(out=b1_sb[net][:], in_=spread1[:].rearrange("r (p t) -> r t p", t=PACK))
+        spread2 = psum_bank.tile([P, 2, CLASSES], F32, name="spread2", tag="bank")
+        nc.tensor.matmul(
+            out=spread2[:].rearrange("r a c -> r (a c)"), lhsT=ones[:], rhs=bias_rows[:, 2 * D_H:],
+            start=True, stop=True,
+        )
+        b2_sb = keep.tile([P, 2, CLASSES], F32, name="b2_sb")
+        nc.vector.tensor_copy(out=b2_sb[:], in_=spread2[:])
+
+        x_codes = keep.tile([P, PASSES, BATCH], U32, name="x_codes", align_bytes=64)
+        x_planes = keep.tile([P, PASSES, BATCH], U8, name="x_planes", align_bytes=64)
+        acc = {}
+        for net in NETS:
+            for rt in range(ROW_TILES):
+                acc[(net, rt)] = psum_acc.tile([P, D_H], F32, name="acc_%s%d" % (net, rt))
+
+        def load_x(r):
+            x_sb = x_pool.tile([P, ROW_TILES, ROUND * K_PASS], BF16, name="x_sb")
+            for rt in range(ROW_TILES):
+                nc.sync.dma_start(
+                    out=x_sb[:, rt, :],
+                    in_=x[rt * P:(rt + 1) * P, r * ROUND * K_PASS:(r + 1) * ROUND * K_PASS],
+                )
+            return x_sb
+
+        def load_w1(net, r):
+            for q in range(QUADRANTS):
+                nc.sync.dma_start(
+                    out=w1_planes[net][32 * q:32 * q + 4 * ROUND, r * D_H:(r + 1) * D_H].bitcast(I32),
+                    in_=w1_scales[net][r * ROUND:(r + 1) * ROUND, 4 * q:4 * q + 4, :].bitcast(I32),
+                )
+            w_sb = w_pool.tile([P, ROUND, D_H], U32, name="w_sb", align_bytes=64)
+            nc.sync.dma_start(
+                out=w_sb[:].bitcast(I32),
+                in_=w1_words[net][r * ROUND:(r + 1) * ROUND].rearrange("g p n t -> p g (n t)").bitcast(I32),
+            )
+            return w_sb
+
+        def transpose_x(x_sb):
+            banks = []
+            for j in range(ROUND):
+                xt = psum_bank.tile([P, 2, BATCH], F32, name="xt", tag="bank")
+                for rt in range(ROW_TILES):
+                    words = x_sb[:, rt, :].bitcast(F32)
+                    for u in range(2):
+                        nc.tensor.transpose(
+                            xt[:, u, rt * P:(rt + 1) * P],
+                            words[:, (K_PASS // 2) * j + u:(K_PASS // 2) * (j + 1):2],
+                            ident_f32[:],
+                        )
+                banks.append(xt)
+            return banks
+
+        def regroup_x(banks):
+            grouped = grouped_pool.tile([P, ROUND, BATCH * PACK], BF16, name="grouped", align_bytes=64)
+            for j in range(ROUND):
+                nc.scalar.copy(
+                    out=grouped[:, j, :].bitcast(F32).rearrange("p (r u) -> p r u", u=2),
+                    in_=banks[j][:].rearrange("p u r -> p r u"),
+                )
+            return grouped
+
+        def quantise_x(r, grouped):
+            passes = slice(r * ROUND, (r + 1) * ROUND)
+            nc.vector.quantize_mx(
+                out=x_codes[:, passes, :].rearrange("p g r -> p (g r)").bitcast(FP8X4),
+                scales=x_planes[:, passes, :].rearrange("p g r -> p (g r)"),
+                in_=grouped[:].rearrange("p g c -> p (g c)"),
+            )
+
+        def layer1_passes(net, r, w_sb):
+            for rt in range(ROW_TILES):
+                rows = slice(rt * P, (rt + 1) * P)
+                for j in range(ROUND):
+                    g = r * ROUND + j
+                    nc.tensor.matmul_mx(
+                        out=acc[(net, rt)][:],
+                        lhsT=x_codes[:, g, rows].bitcast(FP8X4),
+                        lhsT_scale=x_planes[:, g, rows],
+                        rhs=w_sb[:, j, :].bitcast(FP8X4),
+                        rhs_scale=w1_planes[net][4 * j:P, r * D_H:(r + 1) * D_H],
+                        start=(g == 0),
+                        stop=(g == PASSES - 1),
+                    )
+
+        w2_sb = {}
+
+        def load_w2_words():
+            for net in NETS:
+                w2_sb[net] = keep.tile([P, CLASSES], U32, name="w2_" + net, align_bytes=64)
+                nc.sync.dma_start(
+                    out=w2_sb[net][:].bitcast(I32),
+                    in_=w2_words[net][0].rearrange("p n t -> p (n t)").bitcast(I32),
+                )
+
+        def load_w2_scales(i, q):
+            nc.sync.dma_start(
+                out=w2_planes[32 * q:32 * q + 4, i * CLASSES:(i + 1) * CLASSES].bitcast(I32),
+                in_=w2_scales[NETS[i]][0, 4 * q:4 * q + 4, :].bitcast(I32),
+            )
+
+        def hidden_plus_bias(net):
+            h_rows = []
+            for rt in range(ROW_TILES):
+                h_row = keep.tile([P, PACK, P], BF16, name="h_row_%s%d" % (net, rt))
+                nc.vector.tensor_tensor(
+                    out=h_row[:], in0=acc[(net, rt)][:].rearrange("r (p t) -> r t p", t=PACK),
+                    in1=b1_sb[net][:], op=ALU.add,
+                )
+                h_rows.append(h_row)
+            return h_rows
+
+        def quantise_hidden(net, h_rows):
+            h_grouped = keep.tile([P, ROW_TILES, P * PACK], BF16, name="h_grouped_" + net, align_bytes=64)
+            for rt in range(ROW_TILES):
+                h_t = psum_bank.tile([P, PACK, P], BF16, name="h_t", tag="bank")
+                for t in range(PACK):
+                    nc.tensor.transpose(h_t[:, t, :], h_rows[rt][:, t, :], ident_bf16[:])
+                nc.scalar.activation(
+                    out=h_grouped[:, rt, :].rearrange("p (r t) -> p r t", t=PACK),
+                    in_=h_t[:].rearrange("p t r -> p r t"), func=ACT.Relu,
+                )
+            h_codes = keep.tile([P, BATCH], U32, name="h_codes_" + net, align_bytes=64)
+            h_planes = keep.tile([P, BATCH], U8, name="h_planes_" + net, align_bytes=64)
+            nc.vector.quantize_mx(
+                out=h_codes[:].bitcast(FP8X4), scales=h_planes[:],
+                in_=h_grouped[:].rearrange("p a c -> p (a c)"),
+            )
+            return h_codes, h_planes
+
+        def softmax_parts(net, h_codes, h_planes):
+            i = NETS.index(net)
+            logits = psum_bank.tile([P, ROW_TILES, CLASSES], F32, name="logits", tag="bank")
+            for rt in range(ROW_TILES):
+                rows = slice(rt * P, (rt + 1) * P)
+                nc.tensor.matmul_mx(
+                    out=logits[:, rt, :],
+                    lhsT=h_codes[:, rows].bitcast(FP8X4), lhsT_scale=h_planes[:, rows],
+                    rhs=w2_sb[net][:].bitcast(FP8X4),
+                    rhs_scale=w2_planes[:, i * CLASSES:(i + 1) * CLASSES],
+                    start=True, stop=True,
+                )
+            z = keep.tile([P, ROW_TILES, CLASSES], F32, name="z_" + net)
+            nc.vector.tensor_tensor(
+                out=z[:], in0=logits[:], in1=b2_sb[:, i:i + 1, :].to_broadcast([P, ROW_TILES, CLASSES]),
+                op=ALU.add,
+            )
+            neg_max = keep.tile([P, ROW_TILES], F32, name="neg_max_" + net)
+            nc.vector.reduce_max(out=neg_max[:], in_=z[:], axis=AXIS.X, negate=True)
+            e = keep.tile([P, ROW_TILES, CLASSES], F32, name="e_" + net)
+            e_sum = keep.tile([P, ROW_TILES], F32, name="e_sum_" + net)
+            for rt in range(ROW_TILES):
+                nc.scalar.activation(
+                    out=e[:, rt, :], in_=z[:, rt, :], func=ACT.Exp, bias=neg_max[:, rt:rt + 1], scale=1.0,
+                    accum_out=e_sum[:, rt:rt + 1],
+                )
+            inv_sum = keep.tile([P, ROW_TILES], F32, name="inv_sum_" + net)
+            nc.vector.reciprocal(out=inv_sum[:], in_=e_sum[:])
+            return e, inv_sum
+
+        def gate(x1):
+            columns = x1
+            factor = None
+            for i in range(GATE_ROUNDS):
+                two_over_m = 2.0 / (2.0 + TAU * TAU) if i == 0 else 1.0
+                squares = keep.tile([P, ROW_TILES, CLASSES], F32, name="squares_%d" % i)
+                total = keep.tile([P, ROW_TILES], F32, name="total_%d" % i)
+                for rt in range(ROW_TILES):
+                    nc.scalar.activation(
+                        out=squares[:, rt, :], in_=columns[:, rt, :], func=ACT.Square,
+                        scale=(1.0 if factor is None else factor[:, rt:rt + 1]),
+                        accum_out=total[:, rt:rt + 1],
+                    )
+                nc.vector.tensor_tensor(out=gate_last[:], in0=gate_last[:], in1=gate_last[:], op=ALU.mult)
+                nc.vector.tensor_tensor(out=total[:], in0=total[:], in1=gate_last[:], op=ALU.add)
+                b = keep.tile([P, ROW_TILES], F32, name="inv_b_%d" % i)
+                a = keep.tile([P, ROW_TILES], F32, name="inv_a_%d" % i)
+                nc.vector.tensor_scalar(
+                    out=b[:], in0=total[:], scalar1=-two_over_m, scalar2=1.0, op0=ALU.mult, op1=ALU.add
+                )
+                nc.vector.tensor_scalar(out=a[:], in0=b[:], scalar1=1.0, scalar2=None, op0=ALU.add)
+                for step in range(INVERSE_STEPS):
+                    nc.vector.tensor_tensor(out=b[:], in0=b[:], in1=b[:], op=ALU.mult)
+                    nc.vector.scalar_tensor_tensor(
+                        out=a[:], in0=b[:], scalar=1.0, in1=a[:], op0=ALU.add, op1=ALU.mult
+                    )
+                factor = keep.tile([P, ROW_TILES], F32, name="factor_%d" % i)
+                nc.vector.tensor_scalar(out=factor[:], in0=a[:], scalar1=two_over_m, scalar2=None, op0=ALU.mult)
+                nc.vector.tensor_tensor(out=gate_last[:], in0=gate_last[:], in1=factor[:], op=ALU.mult)
+                columns = squares
+            return gate_last
+
+        assert ROUNDS == len(NETS) * QUADRANTS
+        w_o = []
+        x_sb = load_x(0)
+        w_o.append(load_w1("o", 0))
+        load_w2_scales(0, 0)
+        grouped = regroup_x(transpose_x(x_sb))
+        for r in range(1, ROUNDS):
+            x_sb = load_x(r)
+            w_o.append(load_w1("o", r))
+            load_w2_scales(r // QUADRANTS, r % QUADRANTS)
+            banks = transpose_x(x_sb)
+            quantise_x(r - 1, grouped)
+            grouped = regroup_x(banks)
+            layer1_passes("o", r - 1, w_o[r - 1])
+        quantise_x(ROUNDS - 1, grouped)
+        layer1_passes("o", ROUNDS - 1, w_o[ROUNDS - 1])
+
+        load_w2_words()
+        h_rows = hidden_plus_bias("o")
+        layer1_passes("f", 0, load_w1("f", 0))
+        h_codes, h_planes = quantise_hidden("o", h_rows)
+        layer1_passes("f", 1, load_w1("f", 1))
+        e_o, inv_sum_o = softmax_parts("o", h_codes, h_planes)
+        x1 = keep.tile([P, ROW_TILES, CLASSES], F32, name="x1")
+        for rt in range(ROW_TILES):
+            nc.vector.tensor_scalar(
+                out=x1[:, rt, :], in0=e_o[:, rt, :], scalar1=inv_sum_o[:, rt:rt + 1], scalar2=None, op0=ALU.mult
+            )
+        cond = gate(x1)
+        one_minus_cond = keep.tile([P, ROW_TILES], F32, name="one_minus_cond")
+        nc.vector.tensor_scalar(
+            out=one_minus_cond[:], in0=cond[:], scalar1=-1.0, scalar2=1.0, op0=ALU.mult, op1=ALU.add
+        )
+        x1_share = keep.tile([P, ROW_TILES, CLASSES], F32, name="x1_share")
+        for rt in range(ROW_TILES):
+            nc.vector.tensor_scalar(
+                out=x1_share[:, rt, :], in0=x1[:, rt, :], scalar1=one_minus_cond[:, rt:rt + 1], scalar2=None,
+                op0=ALU.mult,
+            )
+        for r in range(2, ROUNDS):
+            layer1_passes("f", r, load_w1("f", r))
+
+        h_codes, h_planes = quantise_hidden("f", hidden_plus_bias("f"))
+        e_f, inv_sum_f = softmax_parts("f", h_codes, h_planes)
+        x2_factor = keep.tile([P, ROW_TILES], F32, name="x2_factor")
+        nc.vector.tensor_tensor(out=x2_factor[:], in0=inv_sum_f[:], in1=cond[:], op=ALU.mult)
+        out_sb = keep.tile([P, ROW_TILES, CLASSES], F32, name="out_sb")
+        for rt in range(ROW_TILES):
+            nc.vector.scalar_tensor_tensor(
+                out=out_sb[:, rt, :], in0=e_f[:, rt, :], scalar=x2_factor[:, rt:rt + 1], in1=x1_share[:, rt, :],
+                op0=ALU.mult, op1=ALU.add,
+            )
+        nc.sync.dma_start(out=out.rearrange("(a p) c -> p a c", p=P), in_=out_sb[:])

@@ -55,7 +55,8 @@ def tile_combnethe_pa_k_kernel(
         w1_planes = {}
         for net in NETS:
             w1_planes[net] = keep.tile([P, ROUNDS * D_H], U8, name="w1_planes_" + net, align_bytes=64)
-        nc.vector.memset(w1_planes["o"][:].bitcast(I32), 0)
+        for net in NETS:
+            nc.vector.memset(w1_planes[net][:].bitcast(I32), 0)
 
         ident_f32 = keep.tile([P, P], F32, name="ident_f32")
         make_identity(nc, ident_f32[:])
@@ -66,36 +67,35 @@ def tile_combnethe_pa_k_kernel(
         nc.vector.memset(bias_rows[:], 0.0)
         ones = keep.tile([P, P], BF16, name="ones")
         nc.vector.memset(ones[:], 1.0)
-        nc.scalar.dma_start(out=bias_rows[0:1, 0:D_H], in_=b1o.rearrange("(a n) -> a n", a=1))
-        nc.scalar.dma_start(out=bias_rows[0:1, D_H:2 * D_H], in_=b1f.rearrange("(a n) -> a n", a=1))
-        nc.scalar.dma_start(
-            out=bias_rows[0:1, 2 * D_H:2 * D_H + CLASSES], in_=b2o.rearrange("(a n) -> a n", a=1)
-        )
-        nc.scalar.dma_start(
-            out=bias_rows[0:1, 2 * D_H + CLASSES:2 * D_H + 2 * CLASSES], in_=b2f.rearrange("(a n) -> a n", a=1)
-        )
 
         w2_planes = keep.tile([P, 2 * CLASSES], U8, name="w2_planes", align_bytes=64)
         nc.vector.memset(w2_planes[:].bitcast(I32), 0)
-        nc.vector.memset(w1_planes["f"][:].bitcast(I32), 0)
         gate_last = keep.tile([P, ROW_TILES], F32, name="gate_last")
         nc.vector.memset(gate_last[:], TAU)
 
         b1_sb = {}
-        for i, net in enumerate(NETS):
-            spread1 = psum_bank.tile([P, D_H], F32, name="spread1", tag="bank")
-            nc.tensor.matmul(
-                out=spread1[:], lhsT=ones[:], rhs=bias_rows[:, i * D_H:(i + 1) * D_H], start=True, stop=True
-            )
-            b1_sb[net] = keep.tile([P, PACK, P], F32, name="b1_" + net)
-            nc.vector.tensor_copy(out=b1_sb[net][:], in_=spread1[:].rearrange("r (p t) -> r t p", t=PACK))
-        spread2 = psum_bank.tile([P, 2, CLASSES], F32, name="spread2", tag="bank")
-        nc.tensor.matmul(
-            out=spread2[:].rearrange("r a c -> r (a c)"), lhsT=ones[:], rhs=bias_rows[:, 2 * D_H:],
-            start=True, stop=True,
-        )
         b2_sb = keep.tile([P, 2, CLASSES], F32, name="b2_sb")
-        nc.vector.tensor_copy(out=b2_sb[:], in_=spread2[:])
+
+        def load_bias(i):
+            vector, start = ((b1o, 0), (b1f, D_H), (b2o, 2 * D_H), (b2f, 2 * D_H + CLASSES))[i]
+            nc.sync.dma_start(
+                out=bias_rows[0:1, start:start + vector.shape[0]], in_=vector.rearrange("(a n) -> a n", a=1)
+            )
+
+        def spread_biases():
+            for i, net in enumerate(NETS):
+                spread1 = psum_bank.tile([P, D_H], F32, name="spread1", tag="bank")
+                nc.tensor.matmul(
+                    out=spread1[:], lhsT=ones[:], rhs=bias_rows[:, i * D_H:(i + 1) * D_H], start=True, stop=True
+                )
+                b1_sb[net] = keep.tile([P, PACK, P], F32, name="b1_" + net)
+                nc.vector.tensor_copy(out=b1_sb[net][:], in_=spread1[:].rearrange("r (p t) -> r t p", t=PACK))
+            spread2 = psum_bank.tile([P, 2, CLASSES], F32, name="spread2", tag="bank")
+            nc.tensor.matmul(
+                out=spread2[:].rearrange("r a c -> r (a c)"), lhsT=ones[:], rhs=bias_rows[:, 2 * D_H:],
+                start=True, stop=True,
+            )
+            nc.vector.tensor_copy(out=b2_sb[:], in_=spread2[:])
 
         x_codes = keep.tile([P, PASSES, BATCH], U32, name="x_codes", align_bytes=64)
         x_planes = keep.tile([P, PASSES, BATCH], U8, name="x_planes", align_bytes=64)
@@ -106,19 +106,21 @@ def tile_combnethe_pa_k_kernel(
 
         def load_x(r):
             x_sb = x_pool.tile([P, ROW_TILES, ROUND * K_PASS], BF16, name="x_sb")
-            for rt in range(ROW_TILES):
-                nc.sync.dma_start(
-                    out=x_sb[:, rt, :],
-                    in_=x[rt * P:(rt + 1) * P, r * ROUND * K_PASS:(r + 1) * ROUND * K_PASS],
-                )
+            columns = x[:, r * ROUND * K_PASS:(r + 1) * ROUND * K_PASS]
+            if r == 0:
+                for rt in range(ROW_TILES):
+                    nc.sync.dma_start(out=x_sb[:, rt, :], in_=columns[rt * P:(rt + 1) * P, :])
+            else:
+                nc.sync.dma_start(out=x_sb[:], in_=columns.rearrange("(a p) k -> p a k", p=P))
             return x_sb
 
+        def load_w1_scales(net, r, q):
+            nc.sync.dma_start(
+                out=w1_planes[net][32 * q:32 * q + 4 * ROUND, r * D_H:(r + 1) * D_H].bitcast(I32),
+                in_=w1_scales[net][r * ROUND:(r + 1) * ROUND, 4 * q:4 * q + 4, :].bitcast(I32),
+            )
+
         def load_w1(net, r):
-            for q in range(QUADRANTS):
-                nc.sync.dma_start(
-                    out=w1_planes[net][32 * q:32 * q + 4 * ROUND, r * D_H:(r + 1) * D_H].bitcast(I32),
-                    in_=w1_scales[net][r * ROUND:(r + 1) * ROUND, 4 * q:4 * q + 4, :].bitcast(I32),
-                )
             w_sb = w_pool.tile([P, ROUND, D_H], U32, name="w_sb", align_bytes=64)
             nc.sync.dma_start(
                 out=w_sb[:].bitcast(I32),
@@ -280,28 +282,55 @@ def tile_combnethe_pa_k_kernel(
                 columns = squares
             return gate_last
 
-        assert ROUNDS == len(NETS) * QUADRANTS
+        EARLY = 12
+        small_f = [(r, q) for r in range(ROUNDS) for q in range(QUADRANTS)]
         w_o = []
-        x_sb = load_x(0)
-        w_o.append(load_w1("o", 0))
-        load_w2_scales(0, 0)
+
+        def load_round_o(r):
+            x_sb = load_x(r)
+            if r == 0:
+                w_o.append(load_w1("o", r))
+            for q in range(2):
+                load_w1_scales("o", r, q)
+            if r < EARLY - ROUNDS:
+                load_w1_scales("f", *small_f.pop(0))
+                load_bias(r)
+            if r > 0:
+                w_o.append(load_w1("o", r))
+            for q in range(2, QUADRANTS):
+                load_w1_scales("o", r, q)
+            load_w1_scales("f", *small_f.pop(0))
+            if r >= EARLY - ROUNDS:
+                load_w2_scales((r - 4) // 2, 2 * (r % 2))
+                load_w2_scales((r - 4) // 2, 2 * (r % 2) + 1)
+            return x_sb
+
+        x_sb = load_round_o(0)
         grouped = regroup_x(transpose_x(x_sb))
         for r in range(1, ROUNDS):
-            x_sb = load_x(r)
-            w_o.append(load_w1("o", r))
-            load_w2_scales(r // QUADRANTS, r % QUADRANTS)
+            x_sb = load_round_o(r)
             banks = transpose_x(x_sb)
             quantise_x(r - 1, grouped)
             grouped = regroup_x(banks)
             layer1_passes("o", r - 1, w_o[r - 1])
+            if r == 5:
+                spread_biases()
         quantise_x(ROUNDS - 1, grouped)
         layer1_passes("o", ROUNDS - 1, w_o[ROUNDS - 1])
 
+        def load_round_f(r):
+            w_sb = load_w1("f", r)
+            for rq in [small_f.pop(0) for i in range(min(3, len(small_f)))]:
+                load_w1_scales("f", *rq)
+            return w_sb
+
+        w_f = [load_round_f(0)]
         load_w2_words()
+        w_f.extend([load_round_f(r) for r in range(1, 3)])
         h_rows = hidden_plus_bias("o")
-        layer1_passes("f", 0, load_w1("f", 0))
+        layer1_passes("f", 0, w_f[0])
         h_codes, h_planes = quantise_hidden("o", h_rows)
-        layer1_passes("f", 1, load_w1("f", 1))
+        layer1_passes("f", 1, w_f[1])
         e_o, inv_sum_o = softmax_parts("o", h_codes, h_planes)
         x1 = keep.tile([P, ROW_TILES, CLASSES], F32, name="x1")
         for rt in range(ROW_TILES):
@@ -320,7 +349,10 @@ def tile_combnethe_pa_k_kernel(
                 op0=ALU.mult,
             )
         for r in range(2, ROUNDS):
-            layer1_passes("f", r, load_w1("f", r))
+            if r + 1 < ROUNDS:
+                w_f.append(load_round_f(r + 1))
+            layer1_passes("f", r, w_f[r])
+        assert not small_f
 
         h_codes, h_planes = quantise_hidden("f", hidden_plus_bias("f"))
         e_f, inv_sum_f = softmax_parts("f", h_codes, h_planes)

@@ -70,8 +70,6 @@ def tile_combnethe_pa_k_kernel(
 
         w2_planes = keep.tile([P, 2 * CLASSES], U8, name="w2_planes", align_bytes=64)
         nc.vector.memset(w2_planes[:].bitcast(I32), 0)
-        gate_last = keep.tile([P, ROW_TILES], F32, name="gate_last")
-        nc.vector.memset(gate_last[:], TAU)
 
         b1_sb = {}
         b2_sb = keep.tile([P, 2, CLASSES], F32, name="b2_sb")
@@ -203,91 +201,124 @@ def tile_combnethe_pa_k_kernel(
             return h_rows
 
         def quantise_hidden(net, h_rows):
-            h_grouped = keep.tile([P, ROW_TILES, P * PACK], BF16, name="h_grouped_" + net, align_bytes=64)
+            grouped = []
             for rt in range(ROW_TILES):
                 h_t = psum_bank.tile([P, PACK, P], BF16, name="h_t", tag="bank")
                 for t in range(PACK):
                     nc.tensor.transpose(h_t[:, t, :], h_rows[rt][:, t, :], ident_bf16[:])
+                h_grouped = keep.tile([P, P * PACK], BF16, name="h_grouped_%s%d" % (net, rt), align_bytes=64)
                 nc.scalar.activation(
-                    out=h_grouped[:, rt, :].rearrange("p (r t) -> p r t", t=PACK),
+                    out=h_grouped[:].rearrange("p (r t) -> p r t", t=PACK),
                     in_=h_t[:].rearrange("p t r -> p r t"), func=ACT.Relu,
                 )
-            h_codes = keep.tile([P, BATCH], U32, name="h_codes_" + net, align_bytes=64)
-            h_planes = keep.tile([P, BATCH], U8, name="h_planes_" + net, align_bytes=64)
-            nc.vector.quantize_mx(
-                out=h_codes[:].bitcast(FP8X4), scales=h_planes[:],
-                in_=h_grouped[:].rearrange("p a c -> p (a c)"),
-            )
-            return h_codes, h_planes
-
-        def softmax_parts(net, h_codes, h_planes):
-            i = NETS.index(net)
-            logits = psum_bank.tile([P, ROW_TILES, CLASSES], F32, name="logits", tag="bank")
+                grouped.append(h_grouped)
+            quantised = []
             for rt in range(ROW_TILES):
-                rows = slice(rt * P, (rt + 1) * P)
+                h_codes = keep.tile([P, P], U32, name="h_codes_%s%d" % (net, rt), align_bytes=64)
+                h_plane = keep.tile([P, P], U8, name="h_plane_%s%d" % (net, rt), align_bytes=64)
+                nc.vector.quantize_mx(out=h_codes[:].bitcast(FP8X4), scales=h_plane[:], in_=grouped[rt][:])
+                quantised.append((h_codes, h_plane))
+            return quantised
+
+        def softmax_parts(net, quantised):
+            i = NETS.index(net)
+            logits, z, neg_max, e, e_sum = [], [], [], [], []
+            for rt in range(ROW_TILES):
+                h_codes, h_plane = quantised[rt]
+                logits.append(psum_bank.tile([P, CLASSES], F32, name="logits", tag="bank"))
                 nc.tensor.matmul_mx(
-                    out=logits[:, rt, :],
-                    lhsT=h_codes[:, rows].bitcast(FP8X4), lhsT_scale=h_planes[:, rows],
+                    out=logits[rt][:],
+                    lhsT=h_codes[:].bitcast(FP8X4), lhsT_scale=h_plane[:],
                     rhs=w2_sb[net][:].bitcast(FP8X4),
                     rhs_scale=w2_planes[:, i * CLASSES:(i + 1) * CLASSES],
                     start=True, stop=True,
                 )
-            z = keep.tile([P, ROW_TILES, CLASSES], F32, name="z_" + net)
-            nc.vector.tensor_tensor(
-                out=z[:], in0=logits[:], in1=b2_sb[:, i:i + 1, :].to_broadcast([P, ROW_TILES, CLASSES]),
-                op=ALU.add,
-            )
-            neg_max = keep.tile([P, ROW_TILES], F32, name="neg_max_" + net)
-            nc.vector.reduce_max(out=neg_max[:], in_=z[:], axis=AXIS.X, negate=True)
-            e = keep.tile([P, ROW_TILES, CLASSES], F32, name="e_" + net)
-            e_sum = keep.tile([P, ROW_TILES], F32, name="e_sum_" + net)
             for rt in range(ROW_TILES):
+                z.append(keep.tile([P, CLASSES], F32, name="z_%s%d" % (net, rt)))
+                nc.vector.tensor_tensor(out=z[rt][:], in0=logits[rt][:], in1=b2_sb[:, i, :], op=ALU.add)
+            for rt in range(ROW_TILES):
+                neg_max.append(keep.tile([P, 1], F32, name="neg_max_%s%d" % (net, rt)))
+                nc.vector.reduce_max(out=neg_max[rt][:], in_=z[rt][:], axis=AXIS.X, negate=True)
+            for rt in range(ROW_TILES):
+                e.append(keep.tile([P, CLASSES], F32, name="e_%s%d" % (net, rt)))
+                e_sum.append(keep.tile([P, 1], F32, name="e_sum_%s%d" % (net, rt)))
                 nc.scalar.activation(
-                    out=e[:, rt, :], in_=z[:, rt, :], func=ACT.Exp, bias=neg_max[:, rt:rt + 1], scale=1.0,
-                    accum_out=e_sum[:, rt:rt + 1],
+                    out=e[rt][:], in_=z[rt][:], func=ACT.Exp, bias=neg_max[rt][:], scale=1.0,
+                    accum_out=e_sum[rt][:],
                 )
-            inv_sum = keep.tile([P, ROW_TILES], F32, name="inv_sum_" + net)
-            nc.vector.reciprocal(out=inv_sum[:], in_=e_sum[:])
-            return e, inv_sum
+            return e, e_sum
 
-        def gate(x1):
-            columns = x1
-            factor = None
+        def gate(e, inv_sum):
+            sums = []
+            columns = e
             for i in range(GATE_ROUNDS):
-                two_over_m = 2.0 / (2.0 + TAU * TAU) if i == 0 else 1.0
-                squares = keep.tile([P, ROW_TILES, CLASSES], F32, name="squares_%d" % i)
-                total = keep.tile([P, ROW_TILES], F32, name="total_%d" % i)
+                total = keep.tile([P, ROW_TILES], F32, name="power_sum_%d" % i)
+                squares = []
                 for rt in range(ROW_TILES):
+                    square = keep.tile([P, CLASSES], F32, name="squares_%d%d" % (i, rt))
                     nc.scalar.activation(
-                        out=squares[:, rt, :], in_=columns[:, rt, :], func=ACT.Square,
-                        scale=(1.0 if factor is None else factor[:, rt:rt + 1]),
-                        accum_out=total[:, rt:rt + 1],
+                        out=square[:], in_=columns[rt][:], func=ACT.Square,
+                        scale=(inv_sum[:, rt:rt + 1] if i == 0 else 1.0), accum_out=total[:, rt:rt + 1],
                     )
-                nc.vector.tensor_tensor(out=gate_last[:], in0=gate_last[:], in1=gate_last[:], op=ALU.mult)
-                nc.vector.tensor_tensor(out=total[:], in0=total[:], in1=gate_last[:], op=ALU.add)
-                b = keep.tile([P, ROW_TILES], F32, name="inv_b_%d" % i)
-                a = keep.tile([P, ROW_TILES], F32, name="inv_a_%d" % i)
+                    squares.append(square)
+                sums.append(total)
+                columns = squares
+
+            def small(name):
+                return keep.tile([P, ROW_TILES], F32, name=name)
+
+            def product(name, in0, in1):
+                result = small(name)
+                nc.vector.tensor_tensor(out=result[:], in0=in0[:], in1=in1[:], op=ALU.mult)
+                return result
+
+            def line(name, in0, factor, shift):
+                result = small(name)
                 nc.vector.tensor_scalar(
-                    out=b[:], in0=total[:], scalar1=-two_over_m, scalar2=1.0, op0=ALU.mult, op1=ALU.add
+                    out=result[:], in0=in0[:], scalar1=factor, scalar2=shift, op0=ALU.mult, op1=ALU.add
                 )
-                nc.vector.tensor_scalar(out=a[:], in0=b[:], scalar1=1.0, scalar2=None, op0=ALU.add)
+                return result
+
+            def inverse(b, a):
                 for step in range(INVERSE_STEPS):
                     nc.vector.tensor_tensor(out=b[:], in0=b[:], in1=b[:], op=ALU.mult)
                     nc.vector.scalar_tensor_tensor(
                         out=a[:], in0=b[:], scalar=1.0, in1=a[:], op0=ALU.add, op1=ALU.mult
                     )
-                factor = keep.tile([P, ROW_TILES], F32, name="factor_%d" % i)
-                nc.vector.tensor_scalar(out=factor[:], in0=a[:], scalar1=two_over_m, scalar2=None, op0=ALU.mult)
-                nc.vector.tensor_tensor(out=gate_last[:], in0=gate_last[:], in1=factor[:], op=ALU.mult)
-                columns = squares
-            return gate_last
+                return a
+
+            c0 = 2.0 / (2.0 + TAU * TAU)
+            b0 = line("gate_b0", sums[0], -c0, 1.0 - c0 * TAU ** 2)
+            a0 = line("gate_a0", sums[0], -c0, 2.0 - c0 * TAU ** 2)
+            inverse(b0, a0)
+            minus4 = line("gate_minus4", sums[1], -(c0 ** 2), -(c0 ** 2) * TAU ** 4)
+            minus8 = line("gate_minus8", sums[2], -(c0 ** 4), -(c0 ** 4) * TAU ** 8)
+            a0_2 = product("gate_a0_2", a0, a0)
+            minus_v1 = product("gate_minus_v1", a0_2, minus4)
+            a0_4 = product("gate_a0_4", a0_2, a0_2)
+            b1 = line("gate_b1", minus_v1, 1.0, 1.0)
+            a1 = line("gate_a1", minus_v1, 1.0, 2.0)
+            inverse(b1, a1)
+            a1_2 = product("gate_a1_2", a1, a1)
+            scale8 = product("gate_scale8", a0_4, a1_2)
+            minus_v2 = product("gate_minus_v2", scale8, minus8)
+            b2 = line("gate_b2", minus_v2, 1.0, 1.0)
+            a2 = line("gate_a2", minus_v2, 1.0, 2.0)
+            inverse(b2, a2)
+            cond = small("cond")
+            nc.vector.scalar_tensor_tensor(
+                out=cond[:], in0=scale8[:], scalar=c0 ** 4 * TAU ** 8, in1=a2[:], op0=ALU.mult, op1=ALU.mult
+            )
+            return cond
 
         EARLY = 12
         small_f = [(r, q) for r in range(ROUNDS) for q in range(QUADRANTS)]
         w_o = []
 
+        x_sb = []
+
         def load_round_o(r):
-            x_sb = load_x(r)
+            x_sb.append(load_x(r))
             if r == 0:
                 w_o.append(load_w1("o", r))
             for q in range(2):
@@ -303,13 +334,12 @@ def tile_combnethe_pa_k_kernel(
             if r >= EARLY - ROUNDS:
                 load_w2_scales((r - 4) // 2, 2 * (r % 2))
                 load_w2_scales((r - 4) // 2, 2 * (r % 2) + 1)
-            return x_sb
 
-        x_sb = load_round_o(0)
-        grouped = regroup_x(transpose_x(x_sb))
+        load_round_o(0)
+        grouped = regroup_x(transpose_x(x_sb[0]))
         for r in range(1, ROUNDS):
-            x_sb = load_round_o(r)
-            banks = transpose_x(x_sb)
+            load_round_o(r)
+            banks = transpose_x(x_sb[r])
             quantise_x(r - 1, grouped)
             grouped = regroup_x(banks)
             layer1_passes("o", r - 1, w_o[r - 1])
@@ -329,24 +359,24 @@ def tile_combnethe_pa_k_kernel(
         w_f.extend([load_round_f(r) for r in range(1, 3)])
         h_rows = hidden_plus_bias("o")
         layer1_passes("f", 0, w_f[0])
-        h_codes, h_planes = quantise_hidden("o", h_rows)
+        quantised = quantise_hidden("o", h_rows)
         layer1_passes("f", 1, w_f[1])
-        e_o, inv_sum_o = softmax_parts("o", h_codes, h_planes)
-        x1 = keep.tile([P, ROW_TILES, CLASSES], F32, name="x1")
+        e_o, e_sum_o = softmax_parts("o", quantised)
+        inv_sum_o = keep.tile([P, ROW_TILES], F32, name="inv_sum_o")
         for rt in range(ROW_TILES):
-            nc.vector.tensor_scalar(
-                out=x1[:, rt, :], in0=e_o[:, rt, :], scalar1=inv_sum_o[:, rt:rt + 1], scalar2=None, op0=ALU.mult
-            )
-        cond = gate(x1)
+            nc.vector.reciprocal(out=inv_sum_o[:, rt:rt + 1], in_=e_sum_o[rt][:])
+        cond = gate(e_o, inv_sum_o)
         one_minus_cond = keep.tile([P, ROW_TILES], F32, name="one_minus_cond")
         nc.vector.tensor_scalar(
             out=one_minus_cond[:], in0=cond[:], scalar1=-1.0, scalar2=1.0, op0=ALU.mult, op1=ALU.add
         )
-        x1_share = keep.tile([P, ROW_TILES, CLASSES], F32, name="x1_share")
+        x1_factor = keep.tile([P, ROW_TILES], F32, name="x1_factor")
+        nc.vector.tensor_tensor(out=x1_factor[:], in0=inv_sum_o[:], in1=one_minus_cond[:], op=ALU.mult)
+        x1_share = []
         for rt in range(ROW_TILES):
+            x1_share.append(keep.tile([P, CLASSES], F32, name="x1_share_%d" % rt))
             nc.vector.tensor_scalar(
-                out=x1_share[:, rt, :], in0=x1[:, rt, :], scalar1=one_minus_cond[:, rt:rt + 1], scalar2=None,
-                op0=ALU.mult,
+                out=x1_share[rt][:], in0=e_o[rt][:], scalar1=x1_factor[:, rt:rt + 1], scalar2=None, op0=ALU.mult
             )
         for r in range(2, ROUNDS):
             if r + 1 < ROUNDS:
@@ -354,14 +384,16 @@ def tile_combnethe_pa_k_kernel(
             layer1_passes("f", r, w_f[r])
         assert not small_f
 
-        h_codes, h_planes = quantise_hidden("f", hidden_plus_bias("f"))
-        e_f, inv_sum_f = softmax_parts("f", h_codes, h_planes)
-        x2_factor = keep.tile([P, ROW_TILES], F32, name="x2_factor")
-        nc.vector.tensor_tensor(out=x2_factor[:], in0=inv_sum_f[:], in1=cond[:], op=ALU.mult)
-        out_sb = keep.tile([P, ROW_TILES, CLASSES], F32, name="out_sb")
+        e_f, e_sum_f = softmax_parts("f", quantise_hidden("f", hidden_plus_bias("f")))
+        x2_factor = []
         for rt in range(ROW_TILES):
+            inv_sum_f = keep.tile([P, 1], F32, name="inv_sum_f%d" % rt)
+            nc.vector.reciprocal(out=inv_sum_f[:], in_=e_sum_f[rt][:])
+            x2_factor.append(keep.tile([P, 1], F32, name="x2_factor_%d" % rt))
+            nc.vector.tensor_tensor(out=x2_factor[rt][:], in0=inv_sum_f[:], in1=cond[:, rt:rt + 1], op=ALU.mult)
+            out_sb = keep.tile([P, CLASSES], F32, name="out_sb%d" % rt)
             nc.vector.scalar_tensor_tensor(
-                out=out_sb[:, rt, :], in0=e_f[:, rt, :], scalar=x2_factor[:, rt:rt + 1], in1=x1_share[:, rt, :],
+                out=out_sb[:], in0=e_f[rt][:], scalar=x2_factor[rt][:], in1=x1_share[rt][:],
                 op0=ALU.mult, op1=ALU.add,
             )
-        nc.sync.dma_start(out=out.rearrange("(a p) c -> p a c", p=P), in_=out_sb[:])
+            nc.sync.dma_start(out=out[rt * P:(rt + 1) * P, :], in_=out_sb[:])

@@ -24,6 +24,8 @@ ROW_TILES = BATCH // P
 PASSES = D_IN // K_PASS
 ROUND = 4
 ROUNDS = PASSES // ROUND
+STEP = 2
+STEPS = PASSES // STEP
 QUADRANTS = 4
 NETS = ("o", "f")
 TAU = 0.5
@@ -126,9 +128,9 @@ def tile_combnethe_pa_k_kernel(
             )
             return w_sb
 
-        def transpose_x(x_sb):
+        def transpose_x(x_sb, first):
             banks = []
-            for j in range(ROUND):
+            for j in range(first, first + STEP):
                 xt = psum_bank.tile([P, 2, BATCH], F32, name="xt", tag="bank")
                 for rt in range(ROW_TILES):
                     words = x_sb[:, rt, :].bitcast(F32)
@@ -142,26 +144,26 @@ def tile_combnethe_pa_k_kernel(
             return banks
 
         def regroup_x(banks):
-            grouped = grouped_pool.tile([P, ROUND, BATCH * PACK], BF16, name="grouped", align_bytes=64)
-            for j in range(ROUND):
+            grouped = grouped_pool.tile([P, STEP, BATCH * PACK], BF16, name="grouped", align_bytes=64)
+            for j in range(STEP):
                 nc.scalar.copy(
                     out=grouped[:, j, :].bitcast(F32).rearrange("p (r u) -> p r u", u=2),
                     in_=banks[j][:].rearrange("p u r -> p r u"),
                 )
             return grouped
 
-        def quantise_x(r, grouped):
-            passes = slice(r * ROUND, (r + 1) * ROUND)
+        def quantise_x(step, grouped):
+            passes = slice(step * STEP, (step + 1) * STEP)
             nc.vector.quantize_mx(
                 out=x_codes[:, passes, :].rearrange("p g r -> p (g r)").bitcast(FP8X4),
                 scales=x_planes[:, passes, :].rearrange("p g r -> p (g r)"),
                 in_=grouped[:].rearrange("p g c -> p (g c)"),
             )
 
-        def layer1_passes(net, r, w_sb):
+        def layer1_passes(net, r, w_sb, passes=range(ROUND)):
             for rt in range(ROW_TILES):
                 rows = slice(rt * P, (rt + 1) * P)
-                for j in range(ROUND):
+                for j in passes:
                     g = r * ROUND + j
                     nc.tensor.matmul_mx(
                         out=acc[(net, rt)][:],
@@ -335,18 +337,24 @@ def tile_combnethe_pa_k_kernel(
                 load_w2_scales((r - 4) // 2, 2 * (r % 2))
                 load_w2_scales((r - 4) // 2, 2 * (r % 2) + 1)
 
+        def multiply_o(step):
+            r, first = step * STEP // ROUND, step * STEP % ROUND
+            layer1_passes("o", r, w_o[r], range(first, first + STEP))
+
         load_round_o(0)
-        grouped = regroup_x(transpose_x(x_sb[0]))
-        for r in range(1, ROUNDS):
-            load_round_o(r)
-            banks = transpose_x(x_sb[r])
-            quantise_x(r - 1, grouped)
+        grouped = regroup_x(transpose_x(x_sb[0], 0))
+        for step in range(1, STEPS):
+            r, first = step * STEP // ROUND, step * STEP % ROUND
+            if first == 0:
+                load_round_o(r)
+            banks = transpose_x(x_sb[r], first)
+            quantise_x(step - 1, grouped)
             grouped = regroup_x(banks)
-            layer1_passes("o", r - 1, w_o[r - 1])
-            if r == 5:
+            multiply_o(step - 1)
+            if step == STEPS - 4:
                 spread_biases()
-        quantise_x(ROUNDS - 1, grouped)
-        layer1_passes("o", ROUNDS - 1, w_o[ROUNDS - 1])
+        quantise_x(STEPS - 1, grouped)
+        multiply_o(STEPS - 1)
 
         def load_round_f(r):
             w_sb = load_w1("f", r)

@@ -28,6 +28,9 @@ STEP = 2
 STEPS = PASSES // STEP
 QUADRANTS = 4
 NETS = ("o", "f")
+WHOLE_ROUND = ((0, 1, 2, 3),)
+LAST_ROUND = ((0, 1), (2,), (3,))
+X_BLOCKS = ((0, 1), (1, 1), (2, 2), (4, 2), (6, 2))
 TAU = 0.5
 GATE_ROUNDS = 3
 INVERSE_STEPS = 3
@@ -48,11 +51,11 @@ def tile_combnethe_pa_k_kernel(
     with ExitStack() as ctx:
         ctx.enter_context(tc.manual_schedule())
         keep = ctx.enter_context(tc.tile_pool(name="keep", bufs=1))
-        x_pool = ctx.enter_context(tc.tile_pool(name="x_pool", bufs=4))
+        x_pool = ctx.enter_context(tc.tile_pool(name="x_pool", bufs=3))
         w_pool = ctx.enter_context(tc.tile_pool(name="w_pool", bufs=10))
         grouped_pool = ctx.enter_context(tc.tile_pool(name="grouped_pool", bufs=2))
         psum_acc = ctx.enter_context(tc.psum_pool(name="psum_acc", bufs=1))
-        psum_bank = ctx.enter_context(tc.psum_pool(name="psum_bank", bufs=4))
+        psum_bank = ctx.enter_context(tc.psum_pool(name="psum_bank", bufs=6))
 
         w1_planes = {}
         for net in NETS:
@@ -100,19 +103,15 @@ def tile_combnethe_pa_k_kernel(
         x_codes = keep.tile([P, PASSES, BATCH], U32, name="x_codes", align_bytes=64)
         x_planes = keep.tile([P, PASSES, BATCH], U8, name="x_planes", align_bytes=64)
         acc = {}
-        for net in NETS:
-            for rt in range(ROW_TILES):
-                acc[(net, rt)] = psum_acc.tile([P, D_H], F32, name="acc_%s%d" % (net, rt))
+        for rt in range(ROW_TILES):
+            acc[("o", rt)] = psum_acc.tile([P, D_H], F32, name="acc_o%d" % rt)
 
-        def load_x(r):
-            x_sb = x_pool.tile([P, ROW_TILES, ROUND * K_PASS], BF16, name="x_sb")
-            columns = x[:, r * ROUND * K_PASS:(r + 1) * ROUND * K_PASS]
-            if r == 0:
-                for rt in range(ROW_TILES):
-                    nc.sync.dma_start(out=x_sb[:, rt, :], in_=columns[rt * P:(rt + 1) * P, :])
-            else:
-                nc.sync.dma_start(out=x_sb[:], in_=columns.rearrange("(a p) k -> p a k", p=P))
-            return x_sb
+        def load_x(x_sb, rt, first, count):
+            width = ROUND * K_PASS
+            nc.sync.dma_start(
+                out=x_sb[:, rt, :count * width],
+                in_=x[rt * P:(rt + 1) * P, first * width:(first + count) * width],
+            )
 
         def load_w1_scales(net, r, q):
             nc.sync.dma_start(
@@ -120,12 +119,14 @@ def tile_combnethe_pa_k_kernel(
                 in_=w1_scales[net][r * ROUND:(r + 1) * ROUND, 4 * q:4 * q + 4, :].bitcast(I32),
             )
 
-        def load_w1(net, r):
+        def load_w1(net, r, parts=WHOLE_ROUND):
             w_sb = w_pool.tile([P, ROUND, D_H], U32, name="w_sb", align_bytes=64)
-            nc.sync.dma_start(
-                out=w_sb[:].bitcast(I32),
-                in_=w1_words[net][r * ROUND:(r + 1) * ROUND].rearrange("g p n t -> p g (n t)").bitcast(I32),
-            )
+            words = w1_words[net][r * ROUND:(r + 1) * ROUND].rearrange("g p n t -> p g (n t)")
+            for part in parts:
+                first, last = part[0], part[-1] + 1
+                nc.sync.dma_start(
+                    out=w_sb[:, first:last, :].bitcast(I32), in_=words[:, first:last, :].bitcast(I32)
+                )
             return w_sb
 
         def transpose_x(x_sb, first):
@@ -143,13 +144,15 @@ def tile_combnethe_pa_k_kernel(
                 banks.append(xt)
             return banks
 
-        def regroup_x(banks):
+        def regroup_x(step, banks):
             grouped = grouped_pool.tile([P, STEP, BATCH * PACK], BF16, name="grouped", align_bytes=64)
             for j in range(STEP):
-                nc.scalar.copy(
-                    out=grouped[:, j, :].bitcast(F32).rearrange("p (r u) -> p r u", u=2),
-                    in_=banks[j][:].rearrange("p u r -> p r u"),
-                )
+                words = grouped[:, j, :].bitcast(F32).rearrange("p (r u) -> p r u", u=2)
+                bank = banks[j][:].rearrange("p u r -> p r u")
+                if (step * STEP + j) % 4 == 3:
+                    nc.vector.tensor_copy(out=words, in_=bank)
+                else:
+                    nc.scalar.copy(out=words, in_=bank)
             return grouped
 
         def quantise_x(step, grouped):
@@ -160,20 +163,21 @@ def tile_combnethe_pa_k_kernel(
                 in_=grouped[:].rearrange("p g c -> p (g c)"),
             )
 
-        def layer1_passes(net, r, w_sb, passes=range(ROUND)):
-            for rt in range(ROW_TILES):
-                rows = slice(rt * P, (rt + 1) * P)
-                for j in passes:
-                    g = r * ROUND + j
-                    nc.tensor.matmul_mx(
-                        out=acc[(net, rt)][:],
-                        lhsT=x_codes[:, g, rows].bitcast(FP8X4),
-                        lhsT_scale=x_planes[:, g, rows],
-                        rhs=w_sb[:, j, :].bitcast(FP8X4),
-                        rhs_scale=w1_planes[net][4 * j:P, r * D_H:(r + 1) * D_H],
-                        start=(g == 0),
-                        stop=(g == PASSES - 1),
-                    )
+        def layer1_passes(net, r, w_sb, parts=WHOLE_ROUND):
+            for part in parts:
+                for rt in range(ROW_TILES):
+                    rows = slice(rt * P, (rt + 1) * P)
+                    for j in part:
+                        g = r * ROUND + j
+                        nc.tensor.matmul_mx(
+                            out=acc[(net, rt)][:],
+                            lhsT=x_codes[:, g, rows].bitcast(FP8X4),
+                            lhsT_scale=x_planes[:, g, rows],
+                            rhs=w_sb[:, j, :].bitcast(FP8X4),
+                            rhs_scale=w1_planes[net][4 * j:P, r * D_H:(r + 1) * D_H],
+                            start=(g == 0),
+                            stop=(g == PASSES - 1),
+                        )
 
         w2_sb = {}
 
@@ -313,58 +317,62 @@ def tile_combnethe_pa_k_kernel(
             )
             return cond
 
-        EARLY = 12
-        small_f = [(r, q) for r in range(ROUNDS) for q in range(QUADRANTS)]
+        small_loads = []
+        for r in range(ROUNDS):
+            for q in range(QUADRANTS):
+                small_loads.append((load_w1_scales, ("o", r, q)))
+        for i in range(4):
+            small_loads.append((load_bias, (i,)))
+        for i in range(len(NETS)):
+            for q in range(QUADRANTS):
+                small_loads.append((load_w2_scales, (i, q)))
+        for r in range(ROUNDS):
+            for q in range(QUADRANTS):
+                small_loads.append((load_w1_scales, ("f", r, q)))
+
+        def load_small(count):
+            for i in range(count):
+                if small_loads:
+                    load, arguments = small_loads.pop(0)
+                    load(*arguments)
+
+        step = 0
+        grouped = []
+        for first, count in X_BLOCKS:
+            x_sb = x_pool.tile([P, ROW_TILES, 2 * ROUND * K_PASS], BF16, name="x_sb")
+            for rt in range(ROW_TILES):
+                load_x(x_sb, rt, first, count)
+                load_small((0, 2, 4)[min(first, 2)])
+            for j in range(0, count * ROUND, STEP):
+                banks = transpose_x(x_sb, j)
+                if step > 0:
+                    quantise_x(step - 1, grouped[step - 1])
+                grouped.append(regroup_x(step, banks))
+                step += 1
+
         w_o = []
-
-        x_sb = []
-
-        def load_round_o(r):
-            x_sb.append(load_x(r))
-            if r == 0:
-                w_o.append(load_w1("o", r))
-            for q in range(2):
-                load_w1_scales("o", r, q)
-            if r < EARLY - ROUNDS:
-                load_w1_scales("f", *small_f.pop(0))
-                load_bias(r)
-            if r > 0:
-                w_o.append(load_w1("o", r))
-            for q in range(2, QUADRANTS):
-                load_w1_scales("o", r, q)
-            load_w1_scales("f", *small_f.pop(0))
-            if r >= EARLY - ROUNDS:
-                load_w2_scales((r - 4) // 2, 2 * (r % 2))
-                load_w2_scales((r - 4) // 2, 2 * (r % 2) + 1)
-
-        def multiply_o(step):
-            r, first = step * STEP // ROUND, step * STEP % ROUND
-            layer1_passes("o", r, w_o[r], range(first, first + STEP))
-
-        load_round_o(0)
-        grouped = regroup_x(transpose_x(x_sb[0], 0))
-        for step in range(1, STEPS):
-            r, first = step * STEP // ROUND, step * STEP % ROUND
-            if first == 0:
-                load_round_o(r)
-            banks = transpose_x(x_sb[r], first)
-            quantise_x(step - 1, grouped)
-            grouped = regroup_x(banks)
-            multiply_o(step - 1)
-            if step == STEPS - 4:
-                spread_biases()
-        quantise_x(STEPS - 1, grouped)
-        multiply_o(STEPS - 1)
+        for r in range(ROUNDS):
+            w_o.append(load_w1("o", r))
+            load_small(4 if r < 3 else 3)
+        load_w2_words()
+        quantise_x(STEPS - 1, grouped[STEPS - 1])
 
         def load_round_f(r):
-            w_sb = load_w1("f", r)
-            for rq in [small_f.pop(0) for i in range(min(3, len(small_f)))]:
-                load_w1_scales("f", *rq)
+            w_sb = load_w1("f", r, LAST_ROUND if r == ROUNDS - 1 else WHOLE_ROUND)
+            load_small(3)
             return w_sb
 
-        w_f = [load_round_f(0)]
-        load_w2_words()
-        w_f.extend([load_round_f(r) for r in range(1, 3)])
+        w_f = [load_round_f(0), load_round_f(1)]
+        for r in range(ROUNDS):
+            layer1_passes("o", r, w_o[r])
+            if r + 2 < ROUNDS:
+                w_f.append(load_round_f(r + 2))
+            if r == ROUNDS // 2:
+                spread_biases()
+        assert not small_loads
+
+        for rt in range(ROW_TILES):
+            acc[("f", rt)] = psum_bank.tile([P, D_H], F32, name="acc_f%d" % rt, tag="bank")
         h_rows = hidden_plus_bias("o")
         layer1_passes("f", 0, w_f[0])
         quantised = quantise_hidden("o", h_rows)
@@ -387,10 +395,7 @@ def tile_combnethe_pa_k_kernel(
                 out=x1_share[rt][:], in0=e_o[rt][:], scalar1=x1_factor[:, rt:rt + 1], scalar2=None, op0=ALU.mult
             )
         for r in range(2, ROUNDS):
-            if r + 1 < ROUNDS:
-                w_f.append(load_round_f(r + 1))
-            layer1_passes("f", r, w_f[r])
-        assert not small_f
+            layer1_passes("f", r, w_f[r], LAST_ROUND if r == ROUNDS - 1 else WHOLE_ROUND)
 
         e_f, e_sum_f = softmax_parts("f", quantise_hidden("f", hidden_plus_bias("f")))
         x2_factor = []

@@ -114,9 +114,9 @@ def tile_combnethe_pa_k_kernel(
             )
 
         def load_w1_scales(net, r, q):
-            nc.sync.dma_start(
-                out=w1_planes[net][32 * q:32 * q + 4 * ROUND, r * D_H:(r + 1) * D_H].bitcast(I32),
-                in_=w1_scales[net][r * ROUND:(r + 1) * ROUND, 4 * q:4 * q + 4, :].bitcast(I32),
+            nc.gpsimd.dma_start(
+                out=w1_planes[net][32 * q:32 * q + 4 * ROUND, r * D_H:(r + 1) * D_H].bitcast(F32),
+                in_=w1_scales[net][r * ROUND:(r + 1) * ROUND, 4 * q:4 * q + 4, :].bitcast(F32),
             )
 
         def load_w1(net, r, parts=WHOLE_ROUND):
@@ -317,18 +317,16 @@ def tile_combnethe_pa_k_kernel(
             )
             return cond
 
+        for net in NETS:
+            for r in range(ROUNDS):
+                for q in range(QUADRANTS):
+                    load_w1_scales(net, r, q)
         small_loads = []
-        for r in range(ROUNDS):
-            for q in range(QUADRANTS):
-                small_loads.append((load_w1_scales, ("o", r, q)))
         for i in range(4):
             small_loads.append((load_bias, (i,)))
         for i in range(len(NETS)):
             for q in range(QUADRANTS):
                 small_loads.append((load_w2_scales, (i, q)))
-        for r in range(ROUNDS):
-            for q in range(QUADRANTS):
-                small_loads.append((load_w1_scales, ("f", r, q)))
 
         def load_small(count):
             for i in range(count):
@@ -342,7 +340,7 @@ def tile_combnethe_pa_k_kernel(
             x_sb = x_pool.tile([P, ROW_TILES, 2 * ROUND * K_PASS], BF16, name="x_sb")
             for rt in range(ROW_TILES):
                 load_x(x_sb, rt, first, count)
-                load_small((0, 2, 4)[min(first, 2)])
+                load_small(min(first, 1))
             for j in range(0, count * ROUND, STEP):
                 banks = transpose_x(x_sb, j)
                 if step > 0:
@@ -353,13 +351,12 @@ def tile_combnethe_pa_k_kernel(
         w_o = []
         for r in range(ROUNDS):
             w_o.append(load_w1("o", r))
-            load_small(4 if r < 3 else 3)
+            load_small(1)
         load_w2_words()
         quantise_x(STEPS - 1, grouped[STEPS - 1])
 
         def load_round_f(r):
             w_sb = load_w1("f", r, LAST_ROUND if r == ROUNDS - 1 else WHOLE_ROUND)
-            load_small(3)
             return w_sb
 
         w_f = [load_round_f(0), load_round_f(1)]

@@ -114,9 +114,10 @@ def tile_combnethe_pa_k_kernel(
             )
 
         def load_w1_scales(net, r, q):
-            nc.gpsimd.dma_start(
-                out=w1_planes[net][32 * q:32 * q + 4 * ROUND, r * D_H:(r + 1) * D_H].bitcast(F32),
-                in_=w1_scales[net][r * ROUND:(r + 1) * ROUND, 4 * q:4 * q + 4, :].bitcast(F32),
+            queue, words = (nc.gpsimd, F32) if net == "o" or r < ROUNDS // 2 else (nc.sync, I32)
+            queue.dma_start(
+                out=w1_planes[net][32 * q:32 * q + 4 * ROUND, r * D_H:(r + 1) * D_H].bitcast(words),
+                in_=w1_scales[net][r * ROUND:(r + 1) * ROUND, 4 * q:4 * q + 4, :].bitcast(words),
             )
 
         def load_w1(net, r, parts=WHOLE_ROUND):
@@ -213,10 +214,12 @@ def tile_combnethe_pa_k_kernel(
                 for t in range(PACK):
                     nc.tensor.transpose(h_t[:, t, :], h_rows[rt][:, t, :], ident_bf16[:])
                 h_grouped = keep.tile([P, P * PACK], BF16, name="h_grouped_%s%d" % (net, rt), align_bytes=64)
-                nc.scalar.activation(
-                    out=h_grouped[:].rearrange("p (r t) -> p r t", t=PACK),
-                    in_=h_t[:].rearrange("p t r -> p r t"), func=ACT.Relu,
-                )
+                words = h_grouped[:].rearrange("p (r t) -> p r t", t=PACK)
+                columns = h_t[:].rearrange("p t r -> p r t")
+                if rt == 0:
+                    nc.scalar.activation(out=words, in_=columns, func=ACT.Relu)
+                else:
+                    nc.vector.tensor_scalar(out=words, in0=columns, scalar1=0.0, scalar2=None, op0=ALU.max)
                 grouped.append(h_grouped)
             quantised = []
             for rt in range(ROW_TILES):
@@ -317,16 +320,21 @@ def tile_combnethe_pa_k_kernel(
             )
             return cond
 
-        for net in NETS:
-            for r in range(ROUNDS):
-                for q in range(QUADRANTS):
-                    load_w1_scales(net, r, q)
+        for r in range(ROUNDS):
+            for q in range(QUADRANTS):
+                load_w1_scales("o", r, q)
+        for r in range(ROUNDS // 2):
+            for q in range(QUADRANTS):
+                load_w1_scales("f", r, q)
         small_loads = []
         for i in range(4):
             small_loads.append((load_bias, (i,)))
         for i in range(len(NETS)):
             for q in range(QUADRANTS):
                 small_loads.append((load_w2_scales, (i, q)))
+        for r in range(ROUNDS // 2, ROUNDS):
+            for q in range(QUADRANTS):
+                small_loads.append((load_w1_scales, ("f", r, q)))
 
         def load_small(count):
             for i in range(count):
@@ -351,7 +359,7 @@ def tile_combnethe_pa_k_kernel(
         w_o = []
         for r in range(ROUNDS):
             w_o.append(load_w1("o", r))
-            load_small(1)
+            load_small(3)
         load_w2_words()
         quantise_x(STEPS - 1, grouped[STEPS - 1])
 

@@ -120,13 +120,12 @@ def tile_combnethe_pa_k_kernel(
                 in_=w1_scales[net][r * ROUND:(r + 1) * ROUND, 4 * q:4 * q + 4, :].bitcast(words),
             )
 
-        def load_w1(net, r, parts=WHOLE_ROUND):
+        def load_w1(net, r):
             w_sb = w_pool.tile([P, ROUND, D_H], U32, name="w_sb", align_bytes=64)
-            words = w1_words[net][r * ROUND:(r + 1) * ROUND].rearrange("g p n t -> p g (n t)")
-            for part in parts:
-                first, last = part[0], part[-1] + 1
+            for j in range(ROUND):
                 nc.sync.dma_start(
-                    out=w_sb[:, first:last, :].bitcast(I32), in_=words[:, first:last, :].bitcast(I32)
+                    out=w_sb[:, j, :].bitcast(I32),
+                    in_=w1_words[net][r * ROUND + j].rearrange("p n t -> p (n t)").bitcast(I32),
                 )
             return w_sb
 
@@ -364,8 +363,7 @@ def tile_combnethe_pa_k_kernel(
         quantise_x(STEPS - 1, grouped[STEPS - 1])
 
         def load_round_f(r):
-            w_sb = load_w1("f", r, LAST_ROUND if r == ROUNDS - 1 else WHOLE_ROUND)
-            return w_sb
+            return load_w1("f", r)
 
         w_f = [load_round_f(0), load_round_f(1)]
         for r in range(ROUNDS):

from contextlib import ExitStack

import concourse.mybir as mybir
from concourse.masks import make_identity

F32 = mybir.dt.float32
BF16 = mybir.dt.bfloat16
I32 = mybir.dt.int32
U32 = mybir.dt.uint32
U8 = mybir.dt.uint8
FP8X4 = mybir.dt.float8_e4m3fn_x4
ALU = mybir.AluOpType
ACT = mybir.ActivationFunctionType
AXIS = mybir.AxisListType

P = 128
PACK = 4
K_PASS = P * PACK
BATCH = 256
D_IN = 16384
D_H = 512
CLASSES = 128
ROW_TILES = BATCH // P
PASSES = D_IN // K_PASS
ROUND = 4
ROUNDS = PASSES // ROUND
STEP = 2
STEPS = PASSES // STEP
QUADRANTS = 4
NETS = ("o", "f")
WHOLE_ROUND = ((0, 1, 2, 3),)
LAST_ROUND = ((0, 1), (2,), (3,))
X_BLOCKS = ((0, 1), (1, 1), (2, 2), (4, 2), (6, 2))
TAU = 0.5
GATE_ROUNDS = 3
INVERSE_STEPS = 3

FLOPS = 2 * BATCH * D_IN * D_H * 2 + 2 * BATCH * D_H * CLASSES * 2


def tile_combnethe_pa_k_kernel(
    tc, x, W1o_words, W1o_scales, b1o, W2o_words, W2o_scales, b2o,
    W1f_words, W1f_scales, b1f, W2f_words, W2f_scales, b2f, out,
):
    nc = tc.nc
    w1_words = {"o": W1o_words, "f": W1f_words}
    w1_scales = {"o": W1o_scales, "f": W1f_scales}
    w2_words = {"o": W2o_words, "f": W2f_words}
    w2_scales = {"o": W2o_scales, "f": W2f_scales}

    with ExitStack() as ctx:
        ctx.enter_context(tc.manual_schedule())
        keep = ctx.enter_context(tc.tile_pool(name="keep", bufs=1))
        x_pool = ctx.enter_context(tc.tile_pool(name="x_pool", bufs=3))
        w_pool = ctx.enter_context(tc.tile_pool(name="w_pool", bufs=10))
        grouped_pool = ctx.enter_context(tc.tile_pool(name="grouped_pool", bufs=2))
        psum_acc = ctx.enter_context(tc.psum_pool(name="psum_acc", bufs=1))
        psum_bank = ctx.enter_context(tc.psum_pool(name="psum_bank", bufs=6))

        w1_planes = {}
        for net in NETS:
            w1_planes[net] = keep.tile([P, ROUNDS * D_H], U8, name="w1_planes_" + net, align_bytes=64)
        for net in NETS:
            nc.vector.memset(w1_planes[net][:].bitcast(I32), 0)

        ident_f32 = keep.tile([P, P], F32, name="ident_f32")
        make_identity(nc, ident_f32[:])
        ident_bf16 = keep.tile([P, P], BF16, name="ident_bf16")
        make_identity(nc, ident_bf16[:])

        bias_rows = keep.tile([P, 2 * D_H + 2 * CLASSES], BF16, name="bias_rows")
        nc.vector.memset(bias_rows[:], 0.0)
        ones = keep.tile([P, P], BF16, name="ones")
        nc.vector.memset(ones[:], 1.0)

        w2_planes = keep.tile([P, 2 * CLASSES], U8, name="w2_planes", align_bytes=64)
        nc.vector.memset(w2_planes[:].bitcast(I32), 0)

        b1_sb = {}
        b2_sb = keep.tile([P, 2, CLASSES], F32, name="b2_sb")

        def load_bias(i):
            vector, start = ((b1o, 0), (b1f, D_H), (b2o, 2 * D_H), (b2f, 2 * D_H + CLASSES))[i]
            nc.sync.dma_start(
                out=bias_rows[0:1, start:start + vector.shape[0]], in_=vector.rearrange("(a n) -> a n", a=1)
            )

        def spread_biases():
            for i, net in enumerate(NETS):
                spread1 = psum_bank.tile([P, D_H], F32, name="spread1", tag="bank")
                nc.tensor.matmul(
                    out=spread1[:], lhsT=ones[:], rhs=bias_rows[:, i * D_H:(i + 1) * D_H], start=True, stop=True
                )
                b1_sb[net] = keep.tile([P, PACK, P], F32, name="b1_" + net)
                nc.vector.tensor_copy(out=b1_sb[net][:], in_=spread1[:].rearrange("r (p t) -> r t p", t=PACK))
            spread2 = psum_bank.tile([P, 2, CLASSES], F32, name="spread2", tag="bank")
            nc.tensor.matmul(
                out=spread2[:].rearrange("r a c -> r (a c)"), lhsT=ones[:], rhs=bias_rows[:, 2 * D_H:],
                start=True, stop=True,
            )
            nc.vector.tensor_copy(out=b2_sb[:], in_=spread2[:])

        x_codes = keep.tile([P, PASSES, BATCH], U32, name="x_codes", align_bytes=64)
        x_planes = keep.tile([P, PASSES, BATCH], U8, name="x_planes", align_bytes=64)
        acc = {}
        for rt in range(ROW_TILES):
            acc[("o", rt)] = psum_acc.tile([P, D_H], F32, name="acc_o%d" % rt)

        def load_x(x_sb, rt, first, count):
            width = ROUND * K_PASS
            nc.sync.dma_start(
                out=x_sb[:, rt, :count * width],
                in_=x[rt * P:(rt + 1) * P, first * width:(first + count) * width],
            )

        def load_w1_scales(net, r, q):
            queue, words = (nc.gpsimd, F32) if net == "o" or r < ROUNDS // 2 else (nc.sync, I32)
            queue.dma_start(
                out=w1_planes[net][32 * q:32 * q + 4 * ROUND, r * D_H:(r + 1) * D_H].bitcast(words),
                in_=w1_scales[net][r * ROUND:(r + 1) * ROUND, 4 * q:4 * q + 4, :].bitcast(words),
            )

        def load_w1(net, r):
            w_sb = w_pool.tile([P, ROUND, D_H], U32, name="w_sb", align_bytes=64)
            for j in range(ROUND):
                nc.sync.dma_start(
                    out=w_sb[:, j, :].bitcast(I32),
                    in_=w1_words[net][r * ROUND + j].rearrange("p n t -> p (n t)").bitcast(I32),
                )
            return w_sb

        def transpose_x(x_sb, first):
            banks = []
            for j in range(first, first + STEP):
                xt = psum_bank.tile([P, 2, BATCH], F32, name="xt", tag="bank")
                for rt in range(ROW_TILES):
                    words = x_sb[:, rt, :].bitcast(F32)
                    for u in range(2):
                        nc.tensor.transpose(
                            xt[:, u, rt * P:(rt + 1) * P],
                            words[:, (K_PASS // 2) * j + u:(K_PASS // 2) * (j + 1):2],
                            ident_f32[:],
                        )
                banks.append(xt)
            return banks

        def regroup_x(step, banks):
            grouped = grouped_pool.tile([P, STEP, BATCH * PACK], BF16, name="grouped", align_bytes=64)
            for j in range(STEP):
                words = grouped[:, j, :].bitcast(F32).rearrange("p (r u) -> p r u", u=2)
                bank = banks[j][:].rearrange("p u r -> p r u")
                if (step * STEP + j) % 4 == 3:
                    nc.vector.tensor_copy(out=words, in_=bank)
                else:
                    nc.scalar.copy(out=words, in_=bank)
            return grouped

        def quantise_x(step, grouped):
            passes = slice(step * STEP, (step + 1) * STEP)
            nc.vector.quantize_mx(
                out=x_codes[:, passes, :].rearrange("p g r -> p (g r)").bitcast(FP8X4),
                scales=x_planes[:, passes, :].rearrange("p g r -> p (g r)"),
                in_=grouped[:].rearrange("p g c -> p (g c)"),
            )

        def layer1_passes(net, r, w_sb, parts=WHOLE_ROUND):
            for part in parts:
                for rt in range(ROW_TILES):
                    rows = slice(rt * P, (rt + 1) * P)
                    for j in part:
                        g = r * ROUND + j
                        nc.tensor.matmul_mx(
                            out=acc[(net, rt)][:],
                            lhsT=x_codes[:, g, rows].bitcast(FP8X4),
                            lhsT_scale=x_planes[:, g, rows],
                            rhs=w_sb[:, j, :].bitcast(FP8X4),
                            rhs_scale=w1_planes[net][4 * j:P, r * D_H:(r + 1) * D_H],
                            start=(g == 0),
                            stop=(g == PASSES - 1),
                        )

        w2_sb = {}

        def load_w2_words():
            for net in NETS:
                w2_sb[net] = keep.tile([P, CLASSES], U32, name="w2_" + net, align_bytes=64)
                nc.sync.dma_start(
                    out=w2_sb[net][:].bitcast(I32),
                    in_=w2_words[net][0].rearrange("p n t -> p (n t)").bitcast(I32),
                )

        def load_w2_scales(i, q):
            nc.sync.dma_start(
                out=w2_planes[32 * q:32 * q + 4, i * CLASSES:(i + 1) * CLASSES].bitcast(I32),
                in_=w2_scales[NETS[i]][0, 4 * q:4 * q + 4, :].bitcast(I32),
            )

        def hidden_plus_bias(net):
            h_rows = []
            for rt in range(ROW_TILES):
                h_row = keep.tile([P, PACK, P], BF16, name="h_row_%s%d" % (net, rt))
                nc.vector.tensor_tensor(
                    out=h_row[:], in0=acc[(net, rt)][:].rearrange("r (p t) -> r t p", t=PACK),
                    in1=b1_sb[net][:], op=ALU.add,
                )
                h_rows.append(h_row)
            return h_rows

        def quantise_hidden(net, h_rows):
            grouped = []
            for rt in range(ROW_TILES):
                h_t = psum_bank.tile([P, PACK, P], BF16, name="h_t", tag="bank")
                for t in range(PACK):
                    nc.tensor.transpose(h_t[:, t, :], h_rows[rt][:, t, :], ident_bf16[:])
                h_grouped = keep.tile([P, P * PACK], BF16, name="h_grouped_%s%d" % (net, rt), align_bytes=64)
                words = h_grouped[:].rearrange("p (r t) -> p r t", t=PACK)
                columns = h_t[:].rearrange("p t r -> p r t")
                if rt == 0:
                    nc.scalar.activation(out=words, in_=columns, func=ACT.Relu)
                else:
                    nc.vector.tensor_scalar(out=words, in0=columns, scalar1=0.0, scalar2=None, op0=ALU.max)
                grouped.append(h_grouped)
            quantised = []
            for rt in range(ROW_TILES):
                h_codes = keep.tile([P, P], U32, name="h_codes_%s%d" % (net, rt), align_bytes=64)
                h_plane = keep.tile([P, P], U8, name="h_plane_%s%d" % (net, rt), align_bytes=64)
                nc.vector.quantize_mx(out=h_codes[:].bitcast(FP8X4), scales=h_plane[:], in_=grouped[rt][:])
                quantised.append((h_codes, h_plane))
            return quantised

        def softmax_parts(net, quantised):
            i = NETS.index(net)
            logits, z, neg_max, e, e_sum = [], [], [], [], []
            for rt in range(ROW_TILES):
                h_codes, h_plane = quantised[rt]
                logits.append(psum_bank.tile([P, CLASSES], F32, name="logits", tag="bank"))
                nc.tensor.matmul_mx(
                    out=logits[rt][:],
                    lhsT=h_codes[:].bitcast(FP8X4), lhsT_scale=h_plane[:],
                    rhs=w2_sb[net][:].bitcast(FP8X4),
                    rhs_scale=w2_planes[:, i * CLASSES:(i + 1) * CLASSES],
                    start=True, stop=True,
                )
            for rt in range(ROW_TILES):
                z.append(keep.tile([P, CLASSES], F32, name="z_%s%d" % (net, rt)))
                nc.vector.tensor_tensor(out=z[rt][:], in0=logits[rt][:], in1=b2_sb[:, i, :], op=ALU.add)
            for rt in range(ROW_TILES):
                neg_max.append(keep.tile([P, 1], F32, name="neg_max_%s%d" % (net, rt)))
                nc.vector.reduce_max(out=neg_max[rt][:], in_=z[rt][:], axis=AXIS.X, negate=True)
            for rt in range(ROW_TILES):
                e.append(keep.tile([P, CLASSES], F32, name="e_%s%d" % (net, rt)))
                e_sum.append(keep.tile([P, 1], F32, name="e_sum_%s%d" % (net, rt)))
                nc.scalar.activation(
                    out=e[rt][:], in_=z[rt][:], func=ACT.Exp, bias=neg_max[rt][:], scale=1.0,
                    accum_out=e_sum[rt][:],
                )
            return e, e_sum

        def gate(e, inv_sum):
            sums = []
            columns = e
            for i in range(GATE_ROUNDS):
                total = keep.tile([P, ROW_TILES], F32, name="power_sum_%d" % i)
                squares = []
                for rt in range(ROW_TILES):
                    square = keep.tile([P, CLASSES], F32, name="squares_%d%d" % (i, rt))
                    nc.scalar.activation(
                        out=square[:], in_=columns[rt][:], func=ACT.Square,
                        scale=(inv_sum[:, rt:rt + 1] if i == 0 else 1.0), accum_out=total[:, rt:rt + 1],
                    )
                    squares.append(square)
                sums.append(total)
                columns = squares

            def small(name):
                return keep.tile([P, ROW_TILES], F32, name=name)

            def product(name, in0, in1):
                result = small(name)
                nc.vector.tensor_tensor(out=result[:], in0=in0[:], in1=in1[:], op=ALU.mult)
                return result

            def line(name, in0, factor, shift):
                result = small(name)
                nc.vector.tensor_scalar(
                    out=result[:], in0=in0[:], scalar1=factor, scalar2=shift, op0=ALU.mult, op1=ALU.add
                )
                return result

            def inverse(b, a):
                for step in range(INVERSE_STEPS):
                    nc.vector.tensor_tensor(out=b[:], in0=b[:], in1=b[:], op=ALU.mult)
                    nc.vector.scalar_tensor_tensor(
                        out=a[:], in0=b[:], scalar=1.0, in1=a[:], op0=ALU.add, op1=ALU.mult
                    )
                return a

            c0 = 2.0 / (2.0 + TAU * TAU)
            b0 = line("gate_b0", sums[0], -c0, 1.0 - c0 * TAU ** 2)
            a0 = line("gate_a0", sums[0], -c0, 2.0 - c0 * TAU ** 2)
            inverse(b0, a0)
            minus4 = line("gate_minus4", sums[1], -(c0 ** 2), -(c0 ** 2) * TAU ** 4)
            minus8 = line("gate_minus8", sums[2], -(c0 ** 4), -(c0 ** 4) * TAU ** 8)
            a0_2 = product("gate_a0_2", a0, a0)
            minus_v1 = product("gate_minus_v1", a0_2, minus4)
            a0_4 = product("gate_a0_4", a0_2, a0_2)
            b1 = line("gate_b1", minus_v1, 1.0, 1.0)
            a1 = line("gate_a1", minus_v1, 1.0, 2.0)
            inverse(b1, a1)
            a1_2 = product("gate_a1_2", a1, a1)
            scale8 = product("gate_scale8", a0_4, a1_2)
            minus_v2 = product("gate_minus_v2", scale8, minus8)
            b2 = line("gate_b2", minus_v2, 1.0, 1.0)
            a2 = line("gate_a2", minus_v2, 1.0, 2.0)
            inverse(b2, a2)
            cond = small("cond")
            nc.vector.scalar_tensor_tensor(
                out=cond[:], in0=scale8[:], scalar=c0 ** 4 * TAU ** 8, in1=a2[:], op0=ALU.mult, op1=ALU.mult
            )
            return cond

        for r in range(ROUNDS):
            for q in range(QUADRANTS):
                load_w1_scales("o", r, q)
        for r in range(ROUNDS // 2):
            for q in range(QUADRANTS):
                load_w1_scales("f", r, q)
        small_loads = []
        for i in range(4):
            small_loads.append((load_bias, (i,)))
        for i in range(len(NETS)):
            for q in range(QUADRANTS):
                small_loads.append((load_w2_scales, (i, q)))
        for r in range(ROUNDS // 2, ROUNDS):
            for q in range(QUADRANTS):
                small_loads.append((load_w1_scales, ("f", r, q)))

        def load_small(count):
            for i in range(count):
                if small_loads:
                    load, arguments = small_loads.pop(0)
                    load(*arguments)

        step = 0
        grouped = []
        for first, count in X_BLOCKS:
            x_sb = x_pool.tile([P, ROW_TILES, 2 * ROUND * K_PASS], BF16, name="x_sb")
            for rt in range(ROW_TILES):
                load_x(x_sb, rt, first, count)
                load_small(min(first, 1))
            for j in range(0, count * ROUND, STEP):
                banks = transpose_x(x_sb, j)
                if step > 0:
                    quantise_x(step - 1, grouped[step - 1])
                grouped.append(regroup_x(step, banks))
                step += 1

        w_o = []
        for r in range(ROUNDS):
            w_o.append(load_w1("o", r))
            load_small(3)
        load_w2_words()
        quantise_x(STEPS - 1, grouped[STEPS - 1])

        def load_round_f(r):
            return load_w1("f", r)

        w_f = [load_round_f(0), load_round_f(1)]
        for r in range(ROUNDS):
            layer1_passes("o", r, w_o[r])
            if r + 2 < ROUNDS:
                w_f.append(load_round_f(r + 2))
            if r == ROUNDS // 2:
                spread_biases()
        assert not small_loads

        for rt in range(ROW_TILES):
            acc[("f", rt)] = psum_bank.tile([P, D_H], F32, name="acc_f%d" % rt, tag="bank")
        h_rows = hidden_plus_bias("o")
        layer1_passes("f", 0, w_f[0])
        quantised = quantise_hidden("o", h_rows)
        layer1_passes("f", 1, w_f[1])
        e_o, e_sum_o = softmax_parts("o", quantised)
        inv_sum_o = keep.tile([P, ROW_TILES], F32, name="inv_sum_o")
        for rt in range(ROW_TILES):
            nc.vector.reciprocal(out=inv_sum_o[:, rt:rt + 1], in_=e_sum_o[rt][:])
        cond = gate(e_o, inv_sum_o)
        one_minus_cond = keep.tile([P, ROW_TILES], F32, name="one_minus_cond")
        nc.vector.tensor_scalar(
            out=one_minus_cond[:], in0=cond[:], scalar1=-1.0, scalar2=1.0, op0=ALU.mult, op1=ALU.add
        )
        x1_factor = keep.tile([P, ROW_TILES], F32, name="x1_factor")
        nc.vector.tensor_tensor(out=x1_factor[:], in0=inv_sum_o[:], in1=one_minus_cond[:], op=ALU.mult)
        x1_share = []
        for rt in range(ROW_TILES):
            x1_share.append(keep.tile([P, CLASSES], F32, name="x1_share_%d" % rt))
            nc.vector.tensor_scalar(
                out=x1_share[rt][:], in0=e_o[rt][:], scalar1=x1_factor[:, rt:rt + 1], scalar2=None, op0=ALU.mult
            )
        for r in range(2, ROUNDS):
            layer1_passes("f", r, w_f[r], LAST_ROUND if r == ROUNDS - 1 else WHOLE_ROUND)

        e_f, e_sum_f = softmax_parts("f", quantise_hidden("f", hidden_plus_bias("f")))
        x2_factor = []
        for rt in range(ROW_TILES):
            inv_sum_f = keep.tile([P, 1], F32, name="inv_sum_f%d" % rt)
            nc.vector.reciprocal(out=inv_sum_f[:], in_=e_sum_f[rt][:])
            x2_factor.append(keep.tile([P, 1], F32, name="x2_factor_%d" % rt))
            nc.vector.tensor_tensor(out=x2_factor[rt][:], in0=inv_sum_f[:], in1=cond[:, rt:rt + 1], op=ALU.mult)
            out_sb = keep.tile([P, CLASSES], F32, name="out_sb%d" % rt)
            nc.vector.scalar_tensor_tensor(
                out=out_sb[:], in0=e_f[rt][:], scalar=x2_factor[rt][:], in1=x1_share[rt][:],
                op0=ALU.mult, op1=ALU.add,
            )
            nc.sync.dma_start(out=out[rt * P:(rt + 1) * P, :], in_=out_sb[:])
